import numpy as np
import ml_dtypes

BF16 = ml_dtypes.bfloat16


def bf(x):
    return np.asarray(x, np.float32).astype(BF16)


def f32(x):
    return np.asarray(x, np.float32)


def f64(x):
    return np.asarray(x).astype(np.float64)


def striped(idx):
    return np.tile(idx.reshape(-1, 16).T, (8, 1))


S, D, M, N, SC, MUL0, MUL1, MUL2, L1, L2 = 1024, 128, 512, 512, 4, 32, 12, 12, 3, 5


def pack(w0, w1, w2):
    t = np.zeros((D, SC, D), np.float32)
    t[:MUL0, :, :MUL0] = w0.transpose(1, 2, 0)
    lo = MUL0
    for wl, mul, dim in ((w1, MUL1, L1), (w2, MUL2, L2)):
        hi = lo + mul * dim
        for r in range(dim):
            t[lo + r:hi:dim, :, lo + r:hi:dim] = wl.transpose(1, 2, 0)
        lo = hi
    return t.reshape(D, M)


def setup_inputs():
    table = bf(np.random.standard_normal((S, D)))
    w0 = np.random.standard_normal((MUL0, MUL0, SC)) / np.sqrt(MUL0)
    w1 = np.random.standard_normal((MUL1, MUL1, SC)) / np.sqrt(MUL1)
    w2 = np.random.standard_normal((MUL2, MUL2, SC)) / np.sqrt(MUL2)
    w = bf(pack(w0, w1, w2))
    x_src = f32(np.random.standard_normal((D, N)))
    return {"table": table, "w": w, "x_src": x_src, "offs": striped(np.random.permutation(np.tile(np.arange(S), 2))[:N])}


def reference(table, w, x_src, offs):
    idx = offs[:16].T.reshape(-1)
    y = f64(w).T @ f64(table)[idx].T
    return (y.reshape(SC, D, N) * f64(x_src)[None]).reshape(M, N)

@@ -1,0 +1,66 @@
+import concourse.mybir as mybir
+from concourse.masks import make_identity
+
+BF16, F32, U16 = mybir.dt.bfloat16, mybir.dt.float32, mybir.dt.uint16
+MULT = mybir.AluOpType.mult
+
+P = 128
+NODES = 1024
+EDGES = 512
+CHANNELS = 4
+NODE_BLOCKS = NODES // P
+FLIPS_PER_BANK = 4
+
+FLOPS = 2 * P * CHANNELS * P * EDGES + CHANNELS * P * EDGES
+
+
+def tile_edgedecoder_kernel(tc, table, w, x_src, offs, out):
+    nc = tc.nc
+    with (
+        tc.tile_pool(name="held", bufs=1) as held,
+        tc.tile_pool(name="products", bufs=CHANNELS) as products,
+        tc.psum_pool(name="flip_psum", bufs=2) as flip_psum,
+        tc.psum_pool(name="pair_psum", bufs=CHANNELS) as pair_psum,
+    ):
+        offsets = held.tile([P, EDGES // 16], U16, name="offsets")
+        nc.sync.dma_start(offsets[:], offs)
+
+        rows = held.tile([P, NODE_BLOCKS, P], BF16, name="rows")
+        table_blocks = table.rearrange("(t p) b -> p t b", p=P)
+        half = NODE_BLOCKS // 2
+        nc.sync.dma_start(rows[:, :half, :], table_blocks[:, :half, :])
+        nc.scalar.dma_start(rows[:, half:, :], table_blocks[:, half:, :])
+
+        weights = held.tile([P, CHANNELS * P], BF16, name="weights")
+        nc.sync.dma_start(weights[:], w)
+        source = held.tile([P, EDGES], F32, name="source")
+        nc.scalar.dma_start(source[:], x_src)
+
+        identity = held.tile([P, P], BF16, name="identity")
+        make_identity(nc, identity[:])
+
+        window = held.tile([P, NODES], BF16, name="window")
+        for bank in range(NODE_BLOCKS // FLIPS_PER_BANK):
+            flipped = flip_psum.tile([P, FLIPS_PER_BANK * P], BF16, name="flipped")
+            for i in range(FLIPS_PER_BANK):
+                t = bank * FLIPS_PER_BANK + i
+                nc.tensor.transpose(flipped[:, i * P : (i + 1) * P], rows[:, t, :], identity[:])
+            columns = window[:, bank * FLIPS_PER_BANK * P : (bank + 1) * FLIPS_PER_BANK * P]
+            if bank % 2 == 0:
+                nc.vector.tensor_copy(columns, flipped[:])
+            else:
+                nc.scalar.copy(columns, flipped[:])
+
+        for k in range(CHANNELS):
+            paired = pair_psum.tile([P, EDGES], F32, name="paired")
+            nc.tensor.matmul(
+                paired[:],
+                weights[:, k * P : (k + 1) * P],
+                window[:].indirect(offsets[:]),
+                start=True,
+                stop=True,
+            )
+            product = products.tile([P, EDGES], F32, name="product")
+            nc.vector.tensor_tensor(product[:], paired[:], source[:], MULT)
+            queue = nc.sync if k % 2 == 0 else nc.scalar
+            queue.dma_start(out[k * P : (k + 1) * P, :], product[:])

@@ -10,6 +10,7 @@ EDGES = 512
 CHANNELS = 4
 NODE_BLOCKS = NODES // P
 FLIPS_PER_BANK = 4
+WARM_MATMULS = 8
 
 FLOPS = 2 * P * CHANNELS * P * EDGES + CHANNELS * P * EDGES
 
@@ -21,6 +22,7 @@ def tile_edgedecoder_kernel(tc, table, w, x_src, offs, out):
         tc.tile_pool(name="products", bufs=CHANNELS) as products,
         tc.psum_pool(name="flip_psum", bufs=2) as flip_psum,
         tc.psum_pool(name="pair_psum", bufs=CHANNELS) as pair_psum,
+        tc.psum_pool(name="warm_psum", bufs=1) as warm_psum,
     ):
         offsets = held.tile([P, EDGES // 16], U16, name="offsets")
         nc.sync.dma_start(offsets[:], offs)
@@ -38,6 +40,12 @@ def tile_edgedecoder_kernel(tc, table, w, x_src, offs, out):
 
         identity = held.tile([P, P], BF16, name="identity")
         make_identity(nc, identity[:])
+
+        zeros = held.tile([P, EDGES], BF16, name="zeros")
+        nc.vector.memset(zeros[:], 0.0)
+        unread = warm_psum.tile([P, EDGES], F32, name="unread")
+        for i in range(WARM_MATMULS):
+            nc.tensor.matmul(unread[:], zeros[:, :P], zeros[:], start=True, stop=True)
 
         window = held.tile([P, NODES], BF16, name="window")
         for bank in range(NODE_BLOCKS // FLIPS_PER_BANK):

@@ -9,8 +9,7 @@ NODES = 1024
 EDGES = 512
 CHANNELS = 4
 NODE_BLOCKS = NODES // P
-FLIPS_PER_BANK = 4
-WARM_MATMULS = 8
+FLIPS_PER_BANK = 2
 
 FLOPS = 2 * P * CHANNELS * P * EDGES + CHANNELS * P * EDGES
 
@@ -20,18 +19,18 @@ def tile_edgedecoder_kernel(tc, table, w, x_src, offs, out):
     with (
         tc.tile_pool(name="held", bufs=1) as held,
         tc.tile_pool(name="products", bufs=CHANNELS) as products,
-        tc.psum_pool(name="flip_psum", bufs=2) as flip_psum,
+        tc.psum_pool(name="flip_psum", bufs=NODE_BLOCKS // FLIPS_PER_BANK) as flip_psum,
         tc.psum_pool(name="pair_psum", bufs=CHANNELS) as pair_psum,
-        tc.psum_pool(name="warm_psum", bufs=1) as warm_psum,
     ):
-        offsets = held.tile([P, EDGES // 16], U16, name="offsets")
-        nc.sync.dma_start(offsets[:], offs)
-
         rows = held.tile([P, NODE_BLOCKS, P], BF16, name="rows")
         table_blocks = table.rearrange("(t p) b -> p t b", p=P)
-        half = NODE_BLOCKS // 2
-        nc.sync.dma_start(rows[:, :half, :], table_blocks[:, :half, :])
-        nc.scalar.dma_start(rows[:, half:, :], table_blocks[:, half:, :])
+        for bank in range(NODE_BLOCKS // FLIPS_PER_BANK):
+            blocks = slice(bank * FLIPS_PER_BANK, (bank + 1) * FLIPS_PER_BANK)
+            queue = nc.sync if bank % 2 == 0 else nc.scalar
+            queue.dma_start(rows[:, blocks, :], table_blocks[:, blocks, :])
+
+        offsets = held.tile([P, EDGES // 16], U16, name="offsets")
+        nc.sync.dma_start(offsets[:], offs)
 
         weights = held.tile([P, CHANNELS * P], BF16, name="weights")
         nc.sync.dma_start(weights[:], w)
@@ -40,12 +39,6 @@ def tile_edgedecoder_kernel(tc, table, w, x_src, offs, out):
 
         identity = held.tile([P, P], BF16, name="identity")
         make_identity(nc, identity[:])
-
-        zeros = held.tile([P, EDGES], BF16, name="zeros")
-        nc.vector.memset(zeros[:], 0.0)
-        unread = warm_psum.tile([P, EDGES], F32, name="unread")
-        for i in range(WARM_MATMULS):
-            nc.tensor.matmul(unread[:], zeros[:, :P], zeros[:], start=True, stop=True)
 
         window = held.tile([P, NODES], BF16, name="window")
         for bank in range(NODE_BLOCKS // FLIPS_PER_BANK):

@@ -8,6 +8,7 @@ P = 128
 NODES = 1024
 EDGES = 512
 CHANNELS = 4
+PIECE = 256
 NODE_BLOCKS = NODES // P
 FLIPS_PER_BANK = 2
 
@@ -18,9 +19,9 @@ def tile_edgedecoder_kernel(tc, table, w, x_src, offs, out):
     nc = tc.nc
     with (
         tc.tile_pool(name="held", bufs=1) as held,
-        tc.tile_pool(name="products", bufs=CHANNELS) as products,
+        tc.tile_pool(name="products", bufs=CHANNELS * (EDGES // PIECE)) as products,
         tc.psum_pool(name="flip_psum", bufs=NODE_BLOCKS // FLIPS_PER_BANK) as flip_psum,
-        tc.psum_pool(name="pair_psum", bufs=CHANNELS) as pair_psum,
+        tc.psum_pool(name="pair_psum", bufs=4) as pair_psum,
     ):
         rows = held.tile([P, NODE_BLOCKS, P], BF16, name="rows")
         table_blocks = table.rearrange("(t p) b -> p t b", p=P)
@@ -47,21 +48,21 @@ def tile_edgedecoder_kernel(tc, table, w, x_src, offs, out):
                 t = bank * FLIPS_PER_BANK + i
                 nc.tensor.transpose(flipped[:, i * P : (i + 1) * P], rows[:, t, :], identity[:])
             columns = window[:, bank * FLIPS_PER_BANK * P : (bank + 1) * FLIPS_PER_BANK * P]
-            if bank % 2 == 0:
-                nc.vector.tensor_copy(columns, flipped[:])
-            else:
-                nc.scalar.copy(columns, flipped[:])
+            nc.vector.tensor_copy(columns, flipped[:])
 
         for k in range(CHANNELS):
-            paired = pair_psum.tile([P, EDGES], F32, name="paired")
-            nc.tensor.matmul(
-                paired[:],
-                weights[:, k * P : (k + 1) * P],
-                window[:].indirect(offsets[:]),
-                start=True,
-                stop=True,
-            )
-            product = products.tile([P, EDGES], F32, name="product")
-            nc.vector.tensor_tensor(product[:], paired[:], source[:], MULT)
-            queue = nc.sync if k % 2 == 0 else nc.scalar
-            queue.dma_start(out[k * P : (k + 1) * P, :], product[:])
+            for piece in range(EDGES // PIECE):
+                edges = slice(piece * PIECE, (piece + 1) * PIECE)
+                piece_offsets = offsets[:, piece * (PIECE // 16) : (piece + 1) * (PIECE // 16)]
+                paired = pair_psum.tile([P, PIECE], F32, name="paired")
+                nc.tensor.matmul(
+                    paired[:],
+                    weights[:, k * P : (k + 1) * P],
+                    window[:].indirect(piece_offsets),
+                    start=True,
+                    stop=True,
+                )
+                product = products.tile([P, PIECE], F32, name="product")
+                nc.vector.tensor_tensor(product[:], paired[:], source[:, edges], MULT)
+                queue = nc.sync if piece % 2 == 0 else nc.scalar
+                queue.dma_start(out[k * P : (k + 1) * P, edges], product[:])

@@ -11,6 +11,7 @@ CHANNELS = 4
 PIECE = 256
 NODE_BLOCKS = NODES // P
 FLIPS_PER_BANK = 2
+WARM_MATMULS = 3
 
 FLOPS = 2 * P * CHANNELS * P * EDGES + CHANNELS * P * EDGES
 
@@ -20,9 +21,16 @@ def tile_edgedecoder_kernel(tc, table, w, x_src, offs, out):
     with (
         tc.tile_pool(name="held", bufs=1) as held,
         tc.tile_pool(name="products", bufs=CHANNELS * (EDGES // PIECE)) as products,
-        tc.psum_pool(name="flip_psum", bufs=NODE_BLOCKS // FLIPS_PER_BANK) as flip_psum,
+        tc.psum_pool(name="flip_psum", bufs=3) as flip_psum,
         tc.psum_pool(name="pair_psum", bufs=4) as pair_psum,
+        tc.psum_pool(name="warm_psum", bufs=1) as warm_psum,
     ):
+        zeros = held.tile([P, EDGES], BF16, name="zeros")
+        nc.gpsimd.memset(zeros[:], 0.0)
+        unread = warm_psum.tile([P, EDGES], F32, name="unread")
+        for i in range(WARM_MATMULS):
+            nc.tensor.matmul(unread[:], zeros[:, :P], zeros[:], start=True, stop=True)
+
         rows = held.tile([P, NODE_BLOCKS, P], BF16, name="rows")
         table_blocks = table.rearrange("(t p) b -> p t b", p=P)
         for bank in range(NODE_BLOCKS // FLIPS_PER_BANK):

@@ -11,6 +11,7 @@ CHANNELS = 4
 PIECE = 256
 NODE_BLOCKS = NODES // P
 FLIPS_PER_BANK = 2
+PSUM_BANKS = 8
 WARM_MATMULS = 3
 
 FLOPS = 2 * P * CHANNELS * P * EDGES + CHANNELS * P * EDGES
@@ -21,13 +22,11 @@ def tile_edgedecoder_kernel(tc, table, w, x_src, offs, out):
     with (
         tc.tile_pool(name="held", bufs=1) as held,
         tc.tile_pool(name="products", bufs=CHANNELS * (EDGES // PIECE)) as products,
-        tc.psum_pool(name="flip_psum", bufs=3) as flip_psum,
-        tc.psum_pool(name="pair_psum", bufs=4) as pair_psum,
-        tc.psum_pool(name="warm_psum", bufs=1) as warm_psum,
+        tc.psum_pool(name="banks", bufs=PSUM_BANKS) as banks,
     ):
         zeros = held.tile([P, EDGES], BF16, name="zeros")
         nc.gpsimd.memset(zeros[:], 0.0)
-        unread = warm_psum.tile([P, EDGES], F32, name="unread")
+        unread = banks.tile([P, EDGES], F32, name="unread", tag="bank")
         for i in range(WARM_MATMULS):
             nc.tensor.matmul(unread[:], zeros[:, :P], zeros[:], start=True, stop=True)
 
@@ -51,7 +50,7 @@ def tile_edgedecoder_kernel(tc, table, w, x_src, offs, out):
 
         window = held.tile([P, NODES], BF16, name="window")
         for bank in range(NODE_BLOCKS // FLIPS_PER_BANK):
-            flipped = flip_psum.tile([P, FLIPS_PER_BANK * P], BF16, name="flipped")
+            flipped = banks.tile([P, FLIPS_PER_BANK * P], BF16, name="flipped", tag="bank")
             for i in range(FLIPS_PER_BANK):
                 t = bank * FLIPS_PER_BANK + i
                 nc.tensor.transpose(flipped[:, i * P : (i + 1) * P], rows[:, t, :], identity[:])
@@ -62,7 +61,7 @@ def tile_edgedecoder_kernel(tc, table, w, x_src, offs, out):
             for piece in range(EDGES // PIECE):
                 edges = slice(piece * PIECE, (piece + 1) * PIECE)
                 piece_offsets = offsets[:, piece * (PIECE // 16) : (piece + 1) * (PIECE // 16)]
-                paired = pair_psum.tile([P, PIECE], F32, name="paired")
+                paired = banks.tile([P, PIECE], F32, name="paired", tag="bank")
                 nc.tensor.matmul(
                     paired[:],
                     weights[:, k * P : (k + 1) * P],

@@ -10,7 +10,7 @@ EDGES = 512
 CHANNELS = 4
 PIECE = 256
 NODE_BLOCKS = NODES // P
-FLIPS_PER_BANK = 2
+PART_BLOCKS = (1, 1, 2, 2, 2)
 PSUM_BANKS = 8
 WARM_MATMULS = 3
 
@@ -32,10 +32,12 @@ def tile_edgedecoder_kernel(tc, table, w, x_src, offs, out):
 
         rows = held.tile([P, NODE_BLOCKS, P], BF16, name="rows")
         table_blocks = table.rearrange("(t p) b -> p t b", p=P)
-        for bank in range(NODE_BLOCKS // FLIPS_PER_BANK):
-            blocks = slice(bank * FLIPS_PER_BANK, (bank + 1) * FLIPS_PER_BANK)
-            queue = nc.sync if bank % 2 == 0 else nc.scalar
+        first_block = 0
+        for part, blocks_in_part in enumerate(PART_BLOCKS):
+            blocks = slice(first_block, first_block + blocks_in_part)
+            queue = nc.sync if part % 2 == 0 else nc.scalar
             queue.dma_start(rows[:, blocks, :], table_blocks[:, blocks, :])
+            first_block += blocks_in_part
 
         offsets = held.tile([P, EDGES // 16], U16, name="offsets")
         nc.sync.dma_start(offsets[:], offs)
@@ -49,13 +51,14 @@ def tile_edgedecoder_kernel(tc, table, w, x_src, offs, out):
         make_identity(nc, identity[:])
 
         window = held.tile([P, NODES], BF16, name="window")
-        for bank in range(NODE_BLOCKS // FLIPS_PER_BANK):
-            flipped = banks.tile([P, FLIPS_PER_BANK * P], BF16, name="flipped", tag="bank")
-            for i in range(FLIPS_PER_BANK):
-                t = bank * FLIPS_PER_BANK + i
-                nc.tensor.transpose(flipped[:, i * P : (i + 1) * P], rows[:, t, :], identity[:])
-            columns = window[:, bank * FLIPS_PER_BANK * P : (bank + 1) * FLIPS_PER_BANK * P]
+        first_block = 0
+        for blocks_in_part in PART_BLOCKS:
+            flipped = banks.tile([P, blocks_in_part * P], BF16, name="flipped", tag="bank")
+            for i in range(blocks_in_part):
+                nc.tensor.transpose(flipped[:, i * P : (i + 1) * P], rows[:, first_block + i, :], identity[:])
+            columns = window[:, first_block * P : (first_block + blocks_in_part) * P]
             nc.vector.tensor_copy(columns, flipped[:])
+            first_block += blocks_in_part
 
         for k in range(CHANNELS):
             for piece in range(EDGES // PIECE):

@@ -10,7 +10,7 @@ EDGES = 512
 CHANNELS = 4
 PIECE = 256
 NODE_BLOCKS = NODES // P
-PART_BLOCKS = (1, 1, 2, 2, 2)
+PART_BLOCKS = (1, 2, 2, 2, 1)
 PSUM_BANKS = 8
 WARM_MATMULS = 3
 
@@ -43,7 +43,7 @@ def tile_edgedecoder_kernel(tc, table, w, x_src, offs, out):
         nc.sync.dma_start(offsets[:], offs)
 
         weights = held.tile([P, CHANNELS * P], BF16, name="weights")
-        nc.sync.dma_start(weights[:], w)
+        nc.scalar.dma_start(weights[:], w)
         source = held.tile([P, EDGES], F32, name="source")
         nc.scalar.dma_start(source[:], x_src)
 

@@ -33,19 +33,18 @@ def tile_edgedecoder_kernel(tc, table, w, x_src, offs, out):
         rows = held.tile([P, NODE_BLOCKS, P], BF16, name="rows")
         table_blocks = table.rearrange("(t p) b -> p t b", p=P)
         first_block = 0
-        for part, blocks_in_part in enumerate(PART_BLOCKS):
+        for blocks_in_part in PART_BLOCKS:
             blocks = slice(first_block, first_block + blocks_in_part)
-            queue = nc.sync if part % 2 == 0 else nc.scalar
-            queue.dma_start(rows[:, blocks, :], table_blocks[:, blocks, :])
+            nc.sync.dma_start(rows[:, blocks, :], table_blocks[:, blocks, :])
             first_block += blocks_in_part
 
         offsets = held.tile([P, EDGES // 16], U16, name="offsets")
         nc.sync.dma_start(offsets[:], offs)
 
         weights = held.tile([P, CHANNELS * P], BF16, name="weights")
-        nc.scalar.dma_start(weights[:], w)
+        nc.sync.dma_start(weights[:], w)
         source = held.tile([P, EDGES], F32, name="source")
-        nc.scalar.dma_start(source[:], x_src)
+        nc.sync.dma_start(source[:], x_src)
 
         identity = held.tile([P, P], BF16, name="identity")
         make_identity(nc, identity[:])
@@ -74,5 +73,4 @@ def tile_edgedecoder_kernel(tc, table, w, x_src, offs, out):
                 )
                 product = products.tile([P, PIECE], F32, name="product")
                 nc.vector.tensor_tensor(product[:], paired[:], source[:, edges], MULT)
-                queue = nc.sync if piece % 2 == 0 else nc.scalar
-                queue.dma_start(out[k * P : (k + 1) * P, edges], product[:])
+                nc.scalar.dma_start(out[k * P : (k + 1) * P, edges], product[:])

@@ -24,11 +24,14 @@ def tile_edgedecoder_kernel(tc, table, w, x_src, offs, out):
         tc.tile_pool(name="products", bufs=CHANNELS * (EDGES // PIECE)) as products,
         tc.psum_pool(name="banks", bufs=PSUM_BANKS) as banks,
     ):
-        zeros = held.tile([P, EDGES], BF16, name="zeros")
-        nc.gpsimd.memset(zeros[:], 0.0)
+        blank = held.tile([P, 2 * P], BF16, name="blank")
+        nc.vector.memset(blank[:], 0.0)
+        identity = blank[:, P:]
+        make_identity(nc, identity, nomemset=True)
+        zeros = blank[:, :P]
         unread = banks.tile([P, EDGES], F32, name="unread", tag="bank")
         for i in range(WARM_MATMULS):
-            nc.tensor.matmul(unread[:], zeros[:, :P], zeros[:], start=True, stop=True)
+            nc.tensor.matmul(unread[:], zeros, blank[:, :1].to_broadcast([P, EDGES]), start=True, stop=True)
 
         rows = held.tile([P, NODE_BLOCKS, P], BF16, name="rows")
         table_blocks = table.rearrange("(t p) b -> p t b", p=P)
@@ -46,15 +49,12 @@ def tile_edgedecoder_kernel(tc, table, w, x_src, offs, out):
         source = held.tile([P, EDGES], F32, name="source")
         nc.sync.dma_start(source[:], x_src)
 
-        identity = held.tile([P, P], BF16, name="identity")
-        make_identity(nc, identity[:])
-
         window = held.tile([P, NODES], BF16, name="window")
         first_block = 0
         for blocks_in_part in PART_BLOCKS:
             flipped = banks.tile([P, blocks_in_part * P], BF16, name="flipped", tag="bank")
             for i in range(blocks_in_part):
-                nc.tensor.transpose(flipped[:, i * P : (i + 1) * P], rows[:, first_block + i, :], identity[:])
+                nc.tensor.transpose(flipped[:, i * P : (i + 1) * P], rows[:, first_block + i, :], identity)
             columns = window[:, first_block * P : (first_block + blocks_in_part) * P]
             nc.vector.tensor_copy(columns, flipped[:])
             first_block += blocks_in_part

import concourse.mybir as mybir
from concourse.masks import make_identity

BF16, F32, U16 = mybir.dt.bfloat16, mybir.dt.float32, mybir.dt.uint16
MULT = mybir.AluOpType.mult

P = 128
NODES = 1024
EDGES = 512
CHANNELS = 4
PIECE = 256
NODE_BLOCKS = NODES // P
PART_BLOCKS = (1, 2, 2, 2, 1)
PSUM_BANKS = 8
WARM_MATMULS = 3

FLOPS = 2 * P * CHANNELS * P * EDGES + CHANNELS * P * EDGES


def tile_edgedecoder_kernel(tc, table, w, x_src, offs, out):
    nc = tc.nc
    with (
        tc.tile_pool(name="held", bufs=1) as held,
        tc.tile_pool(name="products", bufs=CHANNELS * (EDGES // PIECE)) as products,
        tc.psum_pool(name="banks", bufs=PSUM_BANKS) as banks,
    ):
        blank = held.tile([P, 2 * P], BF16, name="blank")
        nc.vector.memset(blank[:], 0.0)
        identity = blank[:, P:]
        make_identity(nc, identity, nomemset=True)
        zeros = blank[:, :P]
        unread = banks.tile([P, EDGES], F32, name="unread", tag="bank")
        for i in range(WARM_MATMULS):
            nc.tensor.matmul(unread[:], zeros, blank[:, :1].to_broadcast([P, EDGES]), start=True, stop=True)

        rows = held.tile([P, NODE_BLOCKS, P], BF16, name="rows")
        table_blocks = table.rearrange("(t p) b -> p t b", p=P)
        first_block = 0
        for blocks_in_part in PART_BLOCKS:
            blocks = slice(first_block, first_block + blocks_in_part)
            nc.sync.dma_start(rows[:, blocks, :], table_blocks[:, blocks, :])
            first_block += blocks_in_part

        offsets = held.tile([P, EDGES // 16], U16, name="offsets")
        nc.sync.dma_start(offsets[:], offs)

        weights = held.tile([P, CHANNELS * P], BF16, name="weights")
        nc.sync.dma_start(weights[:], w)
        source = held.tile([P, EDGES], F32, name="source")
        nc.sync.dma_start(source[:], x_src)

        window = held.tile([P, NODES], BF16, name="window")
        first_block = 0
        for blocks_in_part in PART_BLOCKS:
            flipped = banks.tile([P, blocks_in_part * P], BF16, name="flipped", tag="bank")
            for i in range(blocks_in_part):
                nc.tensor.transpose(flipped[:, i * P : (i + 1) * P], rows[:, first_block + i, :], identity)
            columns = window[:, first_block * P : (first_block + blocks_in_part) * P]
            nc.vector.tensor_copy(columns, flipped[:])
            first_block += blocks_in_part

        for k in range(CHANNELS):
            for piece in range(EDGES // PIECE):
                edges = slice(piece * PIECE, (piece + 1) * PIECE)
                piece_offsets = offsets[:, piece * (PIECE // 16) : (piece + 1) * (PIECE // 16)]
                paired = banks.tile([P, PIECE], F32, name="paired", tag="bank")
                nc.tensor.matmul(
                    paired[:],
                    weights[:, k * P : (k + 1) * P],
                    window[:].indirect(piece_offsets),
                    start=True,
                    stop=True,
                )
                product = products.tile([P, PIECE], F32, name="product")
                nc.vector.tensor_tensor(product[:], paired[:], source[:, edges], MULT)
                nc.scalar.dma_start(out[k * P : (k + 1) * P, edges], product[:])
